import numpy as np
import ml_dtypes

BF16 = ml_dtypes.bfloat16


def bf(x):
    return np.asarray(x, np.float32).astype(BF16)


def f32(x):
    return np.asarray(x, np.float32)


def f64(x):
    return np.asarray(x).astype(np.float64)


def striped(idx):
    return np.tile(idx.reshape(-1, 16).T, (8, 1))


C, C2, CC, S, R, K, N = 512, 1024, 512, 1024, 512, 4, 2048
EPS = 1e-5


def sigmoid(v):
    return 1.0 / (1.0 + np.exp(-v))


def ln_cols(v):
    mu = v.mean(axis=0, keepdims=True)
    var = ((v - mu) * (v - mu)).mean(axis=0, keepdims=True)
    return (v - mu) / np.sqrt(var + EPS)


def setup_inputs():
    return {
        "x": f32(0.3 + 1.5 * np.random.standard_normal((C, N))),
        "cond_embed": f32(-0.2 + 1.3 * np.random.standard_normal((CC, S))),
        "w_ln_cond": f32(1.0 + 0.1 * np.random.standard_normal((CC, 1))),
        "w_cond": bf(np.random.standard_normal((CC, C)) / np.sqrt(CC)),
        "b_cond": f32(0.1 * np.random.standard_normal((C, 1))),
        "w_q": bf(np.random.standard_normal((C, C)) / np.sqrt(C)),
        "w_kv": bf(np.random.standard_normal((C, C2)) / np.sqrt(C)),
        "w_gate": bf(np.random.standard_normal((C, C)) / np.sqrt(C)),
        "offs": striped(np.concatenate([np.random.permutation(S)[:R] for _ in range(K)])),
    }


def reference(x, cond_embed, w_ln_cond, w_cond, b_cond, w_q, w_kv, w_gate, offs):
    idx = offs[:16].T.reshape(-1)
    cn = ln_cols(f64(cond_embed)) * f64(w_ln_cond)
    tab = sigmoid(f64(w_cond).T @ cn + f64(b_cond))
    xn = ln_cols(f64(x))
    s = tab[:, idx] * xn
    q = f64(w_q).T @ s
    kv = f64(w_kv).T @ s
    gt = sigmoid(f64(w_gate).T @ s)
    return np.concatenate([q, kv, gt], axis=0)

@@ -1,0 +1,146 @@
+import concourse.mybir as mybir
+
+F32 = mybir.dt.float32
+BF16 = mybir.dt.bfloat16
+U16 = mybir.dt.uint16
+ALU = mybir.AluOpType
+ACT = mybir.ActivationFunctionType
+
+P = 128
+ROWS = 512
+BLOCKS = ROWS // P
+CONDS = 1024
+NODES = 2048
+PIECE = 512
+Q_ROWS, KV_ROWS, GATE_ROWS = 512, 1024, 512
+OUT_ROWS = Q_ROWS + KV_ROWS + GATE_ROWS
+EPS = 1e-5
+
+FLOPS = 2 * ROWS * ROWS * CONDS + 2 * ROWS * OUT_ROWS * NODES
+
+
+def tile_conditionedblockattentionpairbias_b_kernel(
+    tc, x, cond_embed, w_ln_cond, w_cond, b_cond, w_q, w_kv, w_gate, offs, out
+):
+    nc = tc.nc
+    with (
+        tc.tile_pool(name="held", bufs=1) as held,
+        tc.tile_pool(name="nodes", bufs=NODES // PIECE) as nodes,
+        tc.tile_pool(name="work", bufs=3) as work,
+        tc.tile_pool(name="staged", bufs=6) as staged,
+        tc.psum_pool(name="stats", bufs=3) as stats,
+        tc.psum_pool(name="sums", bufs=5) as sums,
+    ):
+        offsets = held.tile([P, NODES // 16], U16, name="offsets")
+        nc.sync.dma_start(offsets[:], offs)
+
+        ce_rows = cond_embed.rearrange("(p a) t -> p a t", a=BLOCKS)
+        ce = held.tile([P, BLOCKS, CONDS], F32, name="ce")
+        nc.sync.dma_start(ce[:, :, 0:PIECE], ce_rows[:, :, 0:PIECE])
+        ln_gain = held.tile([P, BLOCKS], F32, name="ln_gain")
+        nc.sync.dma_start(ln_gain[:], w_ln_cond.rearrange("(p a) o -> p (a o)", a=BLOCKS))
+        nc.sync.dma_start(ce[:, :, PIECE:CONDS], ce_rows[:, :, PIECE:CONDS])
+        cond_w = held.tile([P, BLOCKS, ROWS], BF16, name="cond_w")
+        nc.sync.dma_start(cond_w[:], w_cond.rearrange("(p a) c -> p a c", a=BLOCKS))
+        cond_bias = held.tile([P, BLOCKS], F32, name="cond_bias")
+        with nc.allow_non_contiguous_dma(reason="one bias value to a partition, 2 KiB in all"):
+            nc.sync.dma_start(cond_bias[:], b_cond.rearrange("(a p) o -> p (a o)", p=P))
+
+        x_rows = x.rearrange("(a p) j -> p a j", p=P)
+        x_pieces = []
+        proj_w = held.tile([P, BLOCKS, OUT_ROWS], BF16, name="proj_w")
+        for k in range(NODES // PIECE):
+            x_k = nodes.tile([P, BLOCKS, PIECE], F32, name="x_k")
+            nc.sync.dma_start(x_k[:], x_rows[:, :, k * PIECE : (k + 1) * PIECE])
+            x_pieces.append(x_k)
+            if k == 0:
+                first = 0
+                for w in (w_q, w_kv, w_gate):
+                    width = w.shape[1]
+                    nc.sync.dma_start(proj_w[:, :, first : first + width], w.rearrange("(a p) m -> p a m", p=P))
+                    first += width
+
+        mean_w = held.tile([P, P], F32, name="mean_w")
+        nc.vector.memset(mean_w[:], 1.0 / ROWS)
+        var_w = held.tile([P, P], BF16, name="var_w")
+        nc.vector.memset(var_w[:], 1.0 / ROWS)
+        eps = held.tile([P, 1], F32, name="eps")
+        nc.vector.memset(eps[:], EPS)
+
+        def deviations_and_rstd(rows, summands):
+            mean = stats.tile([P, PIECE], F32, name="stat")
+            for i, part in enumerate(summands):
+                nc.tensor.matmul(mean[:], mean_w[:], part, start=(i == 0), stop=(i == len(summands) - 1))
+            dev = work.tile([P, BLOCKS, PIECE], F32, name="dev")
+            squares = work.tile([P, BLOCKS, PIECE], BF16, name="squares")
+            var = stats.tile([P, PIECE], F32, name="stat")
+            for a in range(BLOCKS):
+                nc.vector.tensor_tensor(dev[:, a, :], rows[:, a, :], mean[:], ALU.subtract)
+                nc.scalar.activation(squares[:, a, :], dev[:, a, :], ACT.Square)
+                nc.tensor.matmul(var[:], var_w[:], squares[:, a, :], start=(a == 0), stop=(a == BLOCKS - 1))
+            rstd = work.tile([P, PIECE], F32, name="rstd")
+            nc.scalar.activation(rstd[:], var[:], ACT.Abs_reciprocal_sqrt, bias=eps[:])
+            return dev, rstd
+
+        cn = held.tile([P, BLOCKS, CONDS], BF16, name="cn")
+        tab = [held.tile([P, CONDS], F32, name=f"tab{b}") for b in range(BLOCKS)]
+        for h in range(CONDS // PIECE):
+            cols = slice(h * PIECE, (h + 1) * PIECE)
+            dev, rstd = deviations_and_rstd(ce[:, :, cols], [ce[:, a, cols] for a in range(BLOCKS)])
+            for a in range(BLOCKS):
+                nc.vector.scalar_tensor_tensor(
+                    cn[:, a, cols], dev[:, a, :], ln_gain[:, a : a + 1], rstd[:], ALU.mult, ALU.mult
+                )
+            for b in range(BLOCKS):
+                acc = sums.tile([P, PIECE], F32, name="acc")
+                for a in range(BLOCKS):
+                    nc.tensor.matmul(
+                        acc[:], cond_w[:, a, b * P : (b + 1) * P], cn[:, a, cols],
+                        start=(a == 0), stop=(a == BLOCKS - 1),
+                    )
+                nc.scalar.activation(tab[b][:, cols], acc[:], ACT.Sigmoid, bias=cond_bias[:, b : b + 1])
+
+        def normalise(k):
+            x_k = x_pieces[k]
+            halves = work.tile([P, 2, PIECE], F32, name="halves")
+            nc.vector.tensor_tensor(halves[:], x_k[:, 0:2, :], x_k[:, 2:4, :], ALU.add)
+            total = work.tile([P, PIECE], F32, name="total")
+            nc.vector.tensor_tensor(total[:], halves[:, 0, :], halves[:, 1, :], ALU.add)
+            dev, rstd = deviations_and_rstd(x_k, [total[:]])
+            xn = work.tile([P, BLOCKS, PIECE], F32, name="xn")
+            for b in range(BLOCKS):
+                nc.vector.tensor_tensor(xn[:, b, :], dev[:, b, :], rstd[:], ALU.mult)
+            return xn
+
+        def condition(k, xn):
+            piece_offsets = offsets[:, k * (PIECE // 16) : (k + 1) * (PIECE // 16)]
+            s = work.tile([P, BLOCKS, PIECE], BF16, name="s")
+            for b in range(BLOCKS):
+                product = work.tile([P, PIECE], F32, name="product")
+                nc.vector.tensor_tensor(product[:], tab[b][:].indirect(piece_offsets), xn[:, b, :], ALU.mult)
+                nc.scalar.copy(s[:, b, :], product[:])
+            return s
+
+        def project(k, s):
+            for m in range(OUT_ROWS // P):
+                acc = sums.tile([P, PIECE], F32, name="acc")
+                for b in range(BLOCKS):
+                    nc.tensor.matmul(
+                        acc[:], proj_w[:, b, m * P : (m + 1) * P], s[:, b, :],
+                        start=(b == 0), stop=(b == BLOCKS - 1),
+                    )
+                rows_out = staged.tile([P, PIECE], F32, name="rows_out")
+                if m * P >= Q_ROWS + KV_ROWS:
+                    nc.scalar.activation(rows_out[:], acc[:], ACT.Sigmoid)
+                elif m % 2 == 0:
+                    nc.vector.tensor_copy(rows_out[:], acc[:])
+                else:
+                    nc.scalar.copy(rows_out[:], acc[:])
+                nc.sync.dma_start(out[m * P : (m + 1) * P, k * PIECE : (k + 1) * PIECE], rows_out[:])
+
+        s = condition(0, normalise(0))
+        for k in range(NODES // PIECE):
+            xn_next = normalise(k + 1) if k + 1 < NODES // PIECE else None
+            project(k, s)
+            if xn_next is not None:
+                s = condition(k + 1, xn_next)

@@ -18,6 +18,11 @@ EPS = 1e-5
 
 FLOPS = 2 * ROWS * ROWS * CONDS + 2 * ROWS * OUT_ROWS * NODES
 
+STAT_BANKS = 3
+PRODUCT_BANKS = 5
+WORK_DEPTH = 3
+STAGED_DEPTH = PRODUCT_BANKS + 1
+
 
 def tile_conditionedblockattentionpairbias_b_kernel(
     tc, x, cond_embed, w_ln_cond, w_cond, b_cond, w_q, w_kv, w_gate, offs, out
@@ -26,10 +31,10 @@ def tile_conditionedblockattentionpairbias_b_kernel(
     with (
         tc.tile_pool(name="held", bufs=1) as held,
         tc.tile_pool(name="nodes", bufs=NODES // PIECE) as nodes,
-        tc.tile_pool(name="work", bufs=3) as work,
-        tc.tile_pool(name="staged", bufs=6) as staged,
-        tc.psum_pool(name="stats", bufs=3) as stats,
-        tc.psum_pool(name="sums", bufs=5) as sums,
+        tc.tile_pool(name="work", bufs=WORK_DEPTH) as work,
+        tc.tile_pool(name="staged", bufs=STAGED_DEPTH) as staged,
+        tc.psum_pool(name="stats", bufs=STAT_BANKS) as stats,
+        tc.psum_pool(name="products", bufs=PRODUCT_BANKS) as products,
     ):
         offsets = held.tile([P, NODES // 16], U16, name="offsets")
         nc.sync.dma_start(offsets[:], offs)
@@ -43,10 +48,10 @@ def tile_conditionedblockattentionpairbias_b_kernel(
         cond_w = held.tile([P, BLOCKS, ROWS], BF16, name="cond_w")
         nc.sync.dma_start(cond_w[:], w_cond.rearrange("(p a) c -> p a c", a=BLOCKS))
         cond_bias = held.tile([P, BLOCKS], F32, name="cond_bias")
-        with nc.allow_non_contiguous_dma(reason="one bias value to a partition, 2 KiB in all"):
-            nc.sync.dma_start(cond_bias[:], b_cond.rearrange("(a p) o -> p (a o)", p=P))
+        with nc.allow_non_contiguous_dma(reason="one bias value to a partition and block, 2 KiB in all"):
+            nc.sync.dma_start(cond_bias[:], b_cond.rearrange("(b p) o -> p (b o)", p=P))
 
-        x_rows = x.rearrange("(a p) j -> p a j", p=P)
+        x_rows = x.rearrange("(b p) j -> p b j", p=P)
         x_pieces = []
         proj_w = held.tile([P, BLOCKS, OUT_ROWS], BF16, name="proj_w")
         for k in range(NODES // PIECE):
@@ -54,11 +59,13 @@ def tile_conditionedblockattentionpairbias_b_kernel(
             nc.sync.dma_start(x_k[:], x_rows[:, :, k * PIECE : (k + 1) * PIECE])
             x_pieces.append(x_k)
             if k == 0:
-                first = 0
+                first_row = 0
                 for w in (w_q, w_kv, w_gate):
-                    width = w.shape[1]
-                    nc.sync.dma_start(proj_w[:, :, first : first + width], w.rearrange("(a p) m -> p a m", p=P))
-                    first += width
+                    rows_of_w = w.shape[1]
+                    nc.sync.dma_start(
+                        proj_w[:, :, first_row : first_row + rows_of_w], w.rearrange("(b p) m -> p b m", p=P)
+                    )
+                    first_row += rows_of_w
 
         mean_w = held.tile([P, P], F32, name="mean_w")
         nc.vector.memset(mean_w[:], 1.0 / ROWS)
@@ -67,32 +74,40 @@ def tile_conditionedblockattentionpairbias_b_kernel(
         eps = held.tile([P, 1], F32, name="eps")
         nc.vector.memset(eps[:], EPS)
 
-        def deviations_and_rstd(rows, summands):
+        table_loaded = held.tile([P, 1], F32, name="table_loaded")
+        nc.scalar.activation(table_loaded[:], eps[:], ACT.Abs_reciprocal_sqrt)
+
+        def deviations_and_rstd(rows):
+            halves = work.tile([P, 2, PIECE], F32, name="halves")
+            nc.vector.tensor_tensor(halves[:], rows[:, 0:2, :], rows[:, 2:4, :], ALU.add)
+            total = work.tile([P, PIECE], F32, name="total")
+            nc.vector.tensor_tensor(total[:], halves[:, 0, :], halves[:, 1, :], ALU.add)
             mean = stats.tile([P, PIECE], F32, name="stat")
-            for i, part in enumerate(summands):
-                nc.tensor.matmul(mean[:], mean_w[:], part, start=(i == 0), stop=(i == len(summands) - 1))
+            nc.tensor.matmul(mean[:], mean_w[:], total[:], start=True, stop=True)
             dev = work.tile([P, BLOCKS, PIECE], F32, name="dev")
             squares = work.tile([P, BLOCKS, PIECE], BF16, name="squares")
             var = stats.tile([P, PIECE], F32, name="stat")
-            for a in range(BLOCKS):
-                nc.vector.tensor_tensor(dev[:, a, :], rows[:, a, :], mean[:], ALU.subtract)
-                nc.scalar.activation(squares[:, a, :], dev[:, a, :], ACT.Square)
-                nc.tensor.matmul(var[:], var_w[:], squares[:, a, :], start=(a == 0), stop=(a == BLOCKS - 1))
+            for i in range(BLOCKS):
+                nc.vector.tensor_tensor(dev[:, i, :], rows[:, i, :], mean[:], ALU.subtract)
+                nc.scalar.activation(squares[:, i, :], dev[:, i, :], ACT.Square)
+                nc.tensor.matmul(var[:], var_w[:], squares[:, i, :], start=(i == 0), stop=(i == BLOCKS - 1))
             rstd = work.tile([P, PIECE], F32, name="rstd")
             nc.scalar.activation(rstd[:], var[:], ACT.Abs_reciprocal_sqrt, bias=eps[:])
             return dev, rstd
 
+        ce_pieces = [slice(first, first + PIECE) for first in range(0, CONDS, PIECE)]
+        ce_stats = [deviations_and_rstd(ce[:, :, cols]) for cols in ce_pieces]
+        x_stats = deviations_and_rstd(x_pieces[0])
+
         cn = held.tile([P, BLOCKS, CONDS], BF16, name="cn")
         tab = [held.tile([P, CONDS], F32, name=f"tab{b}") for b in range(BLOCKS)]
-        for h in range(CONDS // PIECE):
-            cols = slice(h * PIECE, (h + 1) * PIECE)
-            dev, rstd = deviations_and_rstd(ce[:, :, cols], [ce[:, a, cols] for a in range(BLOCKS)])
+        for cols, (dev, rstd) in zip(ce_pieces, ce_stats):
             for a in range(BLOCKS):
                 nc.vector.scalar_tensor_tensor(
                     cn[:, a, cols], dev[:, a, :], ln_gain[:, a : a + 1], rstd[:], ALU.mult, ALU.mult
                 )
             for b in range(BLOCKS):
-                acc = sums.tile([P, PIECE], F32, name="acc")
+                acc = products.tile([P, PIECE], F32, name="acc")
                 for a in range(BLOCKS):
                     nc.tensor.matmul(
                         acc[:], cond_w[:, a, b * P : (b + 1) * P], cn[:, a, cols],
@@ -100,19 +115,13 @@ def tile_conditionedblockattentionpairbias_b_kernel(
                     )
                 nc.scalar.activation(tab[b][:, cols], acc[:], ACT.Sigmoid, bias=cond_bias[:, b : b + 1])
 
-        def normalise(k):
-            x_k = x_pieces[k]
-            halves = work.tile([P, 2, PIECE], F32, name="halves")
-            nc.vector.tensor_tensor(halves[:], x_k[:, 0:2, :], x_k[:, 2:4, :], ALU.add)
-            total = work.tile([P, PIECE], F32, name="total")
-            nc.vector.tensor_tensor(total[:], halves[:, 0, :], halves[:, 1, :], ALU.add)
-            dev, rstd = deviations_and_rstd(x_k, [total[:]])
+        def normalised(dev, rstd):
             xn = work.tile([P, BLOCKS, PIECE], F32, name="xn")
             for b in range(BLOCKS):
                 nc.vector.tensor_tensor(xn[:, b, :], dev[:, b, :], rstd[:], ALU.mult)
             return xn
 
-        def condition(k, xn):
+        def conditioned(k, xn):
             piece_offsets = offsets[:, k * (PIECE // 16) : (k + 1) * (PIECE // 16)]
             s = work.tile([P, BLOCKS, PIECE], BF16, name="s")
             for b in range(BLOCKS):
@@ -123,7 +132,7 @@ def tile_conditionedblockattentionpairbias_b_kernel(
 
         def project(k, s):
             for m in range(OUT_ROWS // P):
-                acc = sums.tile([P, PIECE], F32, name="acc")
+                acc = products.tile([P, PIECE], F32, name="acc")
                 for b in range(BLOCKS):
                     nc.tensor.matmul(
                         acc[:], proj_w[:, b, m * P : (m + 1) * P], s[:, b, :],
@@ -138,9 +147,11 @@ def tile_conditionedblockattentionpairbias_b_kernel(
                     nc.scalar.copy(rows_out[:], acc[:])
                 nc.sync.dma_start(out[m * P : (m + 1) * P, k * PIECE : (k + 1) * PIECE], rows_out[:])
 
-        s = condition(0, normalise(0))
+        s = conditioned(0, normalised(*x_stats))
         for k in range(NODES // PIECE):
-            xn_next = normalise(k + 1) if k + 1 < NODES // PIECE else None
+            last = k == NODES // PIECE - 1
+            if not last:
+                xn_next = normalised(*deviations_and_rstd(x_pieces[k + 1]))
             project(k, s)
-            if xn_next is not None:
-                s = condition(k + 1, xn_next)
+            if not last:
+                s = conditioned(k + 1, xn_next)

@@ -43,13 +43,13 @@ def tile_conditionedblockattentionpairbias_b_kernel(
         ce = held.tile([P, BLOCKS, CONDS], F32, name="ce")
         nc.sync.dma_start(ce[:, :, 0:PIECE], ce_rows[:, :, 0:PIECE])
         ln_gain = held.tile([P, BLOCKS], F32, name="ln_gain")
-        nc.sync.dma_start(ln_gain[:], w_ln_cond.rearrange("(p a) o -> p (a o)", a=BLOCKS))
+        nc.scalar.dma_start(ln_gain[:], w_ln_cond.rearrange("(p a) o -> p (a o)", a=BLOCKS))
         nc.sync.dma_start(ce[:, :, PIECE:CONDS], ce_rows[:, :, PIECE:CONDS])
         cond_w = held.tile([P, BLOCKS, ROWS], BF16, name="cond_w")
         nc.sync.dma_start(cond_w[:], w_cond.rearrange("(p a) c -> p a c", a=BLOCKS))
         cond_bias = held.tile([P, BLOCKS], F32, name="cond_bias")
         with nc.allow_non_contiguous_dma(reason="one bias value to a partition and block, 2 KiB in all"):
-            nc.sync.dma_start(cond_bias[:], b_cond.rearrange("(b p) o -> p (b o)", p=P))
+            nc.scalar.dma_start(cond_bias[:], b_cond.rearrange("(b p) o -> p (b o)", p=P))
 
         x_rows = x.rearrange("(b p) j -> p b j", p=P)
         x_pieces = []
@@ -115,18 +115,14 @@ def tile_conditionedblockattentionpairbias_b_kernel(
                     )
                 nc.scalar.activation(tab[b][:, cols], acc[:], ACT.Sigmoid, bias=cond_bias[:, b : b + 1])
 
-        def normalised(dev, rstd):
-            xn = work.tile([P, BLOCKS, PIECE], F32, name="xn")
-            for b in range(BLOCKS):
-                nc.vector.tensor_tensor(xn[:, b, :], dev[:, b, :], rstd[:], ALU.mult)
-            return xn
-
-        def conditioned(k, xn):
+        def conditioned(k, dev, rstd):
             piece_offsets = offsets[:, k * (PIECE // 16) : (k + 1) * (PIECE // 16)]
             s = work.tile([P, BLOCKS, PIECE], BF16, name="s")
             for b in range(BLOCKS):
+                xn = work.tile([P, PIECE], F32, name="xn")
+                nc.vector.tensor_tensor(xn[:], dev[:, b, :], rstd[:], ALU.mult)
                 product = work.tile([P, PIECE], F32, name="product")
-                nc.vector.tensor_tensor(product[:], tab[b][:].indirect(piece_offsets), xn[:, b, :], ALU.mult)
+                nc.vector.tensor_tensor(product[:], tab[b][:].indirect(piece_offsets), xn[:], ALU.mult)
                 nc.scalar.copy(s[:, b, :], product[:])
             return s
 
@@ -147,11 +143,11 @@ def tile_conditionedblockattentionpairbias_b_kernel(
                     nc.scalar.copy(rows_out[:], acc[:])
                 nc.sync.dma_start(out[m * P : (m + 1) * P, k * PIECE : (k + 1) * PIECE], rows_out[:])
 
-        s = conditioned(0, normalised(*x_stats))
+        s = conditioned(0, *x_stats)
         for k in range(NODES // PIECE):
             last = k == NODES // PIECE - 1
             if not last:
-                xn_next = normalised(*deviations_and_rstd(x_pieces[k + 1]))
+                x_stats = deviations_and_rstd(x_pieces[k + 1])
             project(k, s)
             if not last:
-                s = conditioned(k + 1, xn_next)
+                s = conditioned(k + 1, *x_stats)

@@ -117,12 +117,13 @@ def tile_conditionedblockattentionpairbias_b_kernel(
 
         def conditioned(k, dev, rstd):
             piece_offsets = offsets[:, k * (PIECE // 16) : (k + 1) * (PIECE // 16)]
+            xn = work.tile([P, BLOCKS, PIECE], F32, name="xn")
+            for b in range(BLOCKS):
+                nc.vector.tensor_tensor(xn[:, b, :], dev[:, b, :], rstd[:], ALU.mult)
             s = work.tile([P, BLOCKS, PIECE], BF16, name="s")
             for b in range(BLOCKS):
-                xn = work.tile([P, PIECE], F32, name="xn")
-                nc.vector.tensor_tensor(xn[:], dev[:, b, :], rstd[:], ALU.mult)
                 product = work.tile([P, PIECE], F32, name="product")
-                nc.vector.tensor_tensor(product[:], tab[b][:].indirect(piece_offsets), xn[:], ALU.mult)
+                nc.vector.tensor_tensor(product[:], tab[b][:].indirect(piece_offsets), xn[:, b, :], ALU.mult)
                 nc.scalar.copy(s[:, b, :], product[:])
             return s
 

@@ -20,6 +20,7 @@ FLOPS = 2 * ROWS * ROWS * CONDS + 2 * ROWS * OUT_ROWS * NODES
 
 STAT_BANKS = 3
 PRODUCT_BANKS = 5
+EARLY_PIECES = 2
 WORK_DEPTH = 3
 STAGED_DEPTH = PRODUCT_BANKS + 1
 
@@ -30,7 +31,8 @@ def tile_conditionedblockattentionpairbias_b_kernel(
     nc = tc.nc
     with (
         tc.tile_pool(name="held", bufs=1) as held,
-        tc.tile_pool(name="nodes", bufs=NODES // PIECE) as nodes,
+        tc.tile_pool(name="nodes", bufs=EARLY_PIECES) as nodes,
+        tc.tile_pool(name="late", bufs=1) as late,
         tc.tile_pool(name="work", bufs=WORK_DEPTH) as work,
         tc.tile_pool(name="staged", bufs=STAGED_DEPTH) as staged,
         tc.psum_pool(name="stats", bufs=STAT_BANKS) as stats,
@@ -54,7 +56,7 @@ def tile_conditionedblockattentionpairbias_b_kernel(
         x_rows = x.rearrange("(b p) j -> p b j", p=P)
         x_pieces = []
         proj_w = held.tile([P, BLOCKS, OUT_ROWS], BF16, name="proj_w")
-        for k in range(NODES // PIECE):
+        for k in range(EARLY_PIECES):
             x_k = nodes.tile([P, BLOCKS, PIECE], F32, name="x_k")
             nc.sync.dma_start(x_k[:], x_rows[:, :, k * PIECE : (k + 1) * PIECE])
             x_pieces.append(x_k)
@@ -99,7 +101,7 @@ def tile_conditionedblockattentionpairbias_b_kernel(
         ce_stats = [deviations_and_rstd(ce[:, :, cols]) for cols in ce_pieces]
         x_stats = deviations_and_rstd(x_pieces[0])
 
-        cn = held.tile([P, BLOCKS, CONDS], BF16, name="cn")
+        cn = late.tile([P, BLOCKS, CONDS], BF16, tag="late", name="cn")
         tab = [held.tile([P, CONDS], F32, name=f"tab{b}") for b in range(BLOCKS)]
         for cols, (dev, rstd) in zip(ce_pieces, ce_stats):
             for a in range(BLOCKS):
@@ -114,6 +116,11 @@ def tile_conditionedblockattentionpairbias_b_kernel(
                         start=(a == 0), stop=(a == BLOCKS - 1),
                     )
                 nc.scalar.activation(tab[b][:, cols], acc[:], ACT.Sigmoid, bias=cond_bias[:, b : b + 1])
+
+        for k in range(EARLY_PIECES, NODES // PIECE):
+            x_k = late.tile([P, BLOCKS, PIECE], F32, tag="late", name="x_k")
+            nc.sync.dma_start(x_k[:], x_rows[:, :, k * PIECE : (k + 1) * PIECE])
+            x_pieces.append(x_k)
 
         def conditioned(k, dev, rstd):
             piece_offsets = offsets[:, k * (PIECE // 16) : (k + 1) * (PIECE // 16)]

@@ -134,22 +134,31 @@ def tile_conditionedblockattentionpairbias_b_kernel(
                 nc.scalar.copy(s[:, b, :], product[:])
             return s
 
+        def project_block(k, s, m, first, width):
+            acc = products.tile([P, width], F32, name="acc")
+            for b in range(BLOCKS):
+                nc.tensor.matmul(
+                    acc[:], proj_w[:, b, m * P : (m + 1) * P], s[:, b, first : first + width],
+                    start=(b == 0), stop=(b == BLOCKS - 1),
+                )
+            rows_out = staged.tile([P, width], F32, name="rows_out")
+            if m * P >= Q_ROWS + KV_ROWS:
+                nc.scalar.activation(rows_out[:], acc[:], ACT.Sigmoid)
+            elif m % 2 == 0:
+                nc.vector.tensor_copy(rows_out[:], acc[:])
+            else:
+                nc.scalar.copy(rows_out[:], acc[:])
+            nc.sync.dma_start(
+                out[m * P : (m + 1) * P, k * PIECE + first : k * PIECE + first + width], rows_out[:]
+            )
+
         def project(k, s):
             for m in range(OUT_ROWS // P):
-                acc = products.tile([P, PIECE], F32, name="acc")
-                for b in range(BLOCKS):
-                    nc.tensor.matmul(
-                        acc[:], proj_w[:, b, m * P : (m + 1) * P], s[:, b, :],
-                        start=(b == 0), stop=(b == BLOCKS - 1),
-                    )
-                rows_out = staged.tile([P, PIECE], F32, name="rows_out")
-                if m * P >= Q_ROWS + KV_ROWS:
-                    nc.scalar.activation(rows_out[:], acc[:], ACT.Sigmoid)
-                elif m % 2 == 0:
-                    nc.vector.tensor_copy(rows_out[:], acc[:])
+                if k == NODES // PIECE - 1 and m == OUT_ROWS // P - 1:
+                    project_block(k, s, m, 0, PIECE // 2)
+                    project_block(k, s, m, PIECE // 2, PIECE // 2)
                 else:
-                    nc.scalar.copy(rows_out[:], acc[:])
-                nc.sync.dma_start(out[m * P : (m + 1) * P, k * PIECE : (k + 1) * PIECE], rows_out[:])
+                    project_block(k, s, m, 0, PIECE)
 
         s = conditioned(0, *x_stats)
         for k in range(NODES // PIECE):

@@ -20,6 +20,7 @@ FLOPS = 2 * ROWS * ROWS * CONDS + 2 * ROWS * OUT_ROWS * NODES
 
 STAT_BANKS = 3
 PRODUCT_BANKS = 5
+LAST_CUT = 4
 EARLY_PIECES = 2
 WORK_DEPTH = 3
 STAGED_DEPTH = PRODUCT_BANKS + 1
@@ -155,8 +156,8 @@ def tile_conditionedblockattentionpairbias_b_kernel(
         def project(k, s):
             for m in range(OUT_ROWS // P):
                 if k == NODES // PIECE - 1 and m == OUT_ROWS // P - 1:
-                    project_block(k, s, m, 0, PIECE // 2)
-                    project_block(k, s, m, PIECE // 2, PIECE // 2)
+                    for first in range(0, PIECE, PIECE // LAST_CUT):
+                        project_block(k, s, m, first, PIECE // LAST_CUT)
                 else:
                     project_block(k, s, m, 0, PIECE)
 

@@ -23,6 +23,7 @@ PRODUCT_BANKS = 5
 LAST_CUT = 4
 EARLY_PIECES = 2
 WORK_DEPTH = 3
+VECTOR_COPY_EVERY = 6
 STAGED_DEPTH = PRODUCT_BANKS + 1
 
 
@@ -80,7 +81,7 @@ def tile_conditionedblockattentionpairbias_b_kernel(
         table_loaded = held.tile([P, 1], F32, name="table_loaded")
         nc.scalar.activation(table_loaded[:], eps[:], ACT.Abs_reciprocal_sqrt)
 
-        def deviations_and_rstd(rows):
+        def deviations_and_rstd(rows, vector_adds_squares):
             halves = work.tile([P, 2, PIECE], F32, name="halves")
             nc.vector.tensor_tensor(halves[:], rows[:, 0:2, :], rows[:, 2:4, :], ALU.add)
             total = work.tile([P, PIECE], F32, name="total")
@@ -93,14 +94,21 @@ def tile_conditionedblockattentionpairbias_b_kernel(
             for i in range(BLOCKS):
                 nc.vector.tensor_tensor(dev[:, i, :], rows[:, i, :], mean[:], ALU.subtract)
                 nc.scalar.activation(squares[:, i, :], dev[:, i, :], ACT.Square)
-                nc.tensor.matmul(var[:], var_w[:], squares[:, i, :], start=(i == 0), stop=(i == BLOCKS - 1))
+                if not vector_adds_squares:
+                    nc.tensor.matmul(var[:], var_w[:], squares[:, i, :], start=(i == 0), stop=(i == BLOCKS - 1))
+            if vector_adds_squares:
+                pairs = work.tile([P, 2, PIECE], BF16, name="pairs")
+                nc.vector.tensor_tensor(pairs[:], squares[:, 0:2, :], squares[:, 2:4, :], ALU.add)
+                sum_of_squares = work.tile([P, PIECE], BF16, name="sum_of_squares")
+                nc.vector.tensor_tensor(sum_of_squares[:], pairs[:, 0, :], pairs[:, 1, :], ALU.add)
+                nc.tensor.matmul(var[:], var_w[:], sum_of_squares[:], start=True, stop=True)
             rstd = work.tile([P, PIECE], F32, name="rstd")
             nc.scalar.activation(rstd[:], var[:], ACT.Abs_reciprocal_sqrt, bias=eps[:])
             return dev, rstd
 
         ce_pieces = [slice(first, first + PIECE) for first in range(0, CONDS, PIECE)]
-        ce_stats = [deviations_and_rstd(ce[:, :, cols]) for cols in ce_pieces]
-        x_stats = deviations_and_rstd(x_pieces[0])
+        ce_stats = [deviations_and_rstd(ce[:, :, cols], vector_adds_squares=False) for cols in ce_pieces]
+        x_stats = deviations_and_rstd(x_pieces[0], vector_adds_squares=False)
 
         cn = late.tile([P, BLOCKS, CONDS], BF16, tag="late", name="cn")
         tab = [held.tile([P, CONDS], F32, name=f"tab{b}") for b in range(BLOCKS)]
@@ -132,7 +140,10 @@ def tile_conditionedblockattentionpairbias_b_kernel(
             for b in range(BLOCKS):
                 product = work.tile([P, PIECE], F32, name="product")
                 nc.vector.tensor_tensor(product[:], tab[b][:].indirect(piece_offsets), xn[:, b, :], ALU.mult)
-                nc.scalar.copy(s[:, b, :], product[:])
+                if k == 0:
+                    nc.scalar.copy(s[:, b, :], product[:])
+                else:
+                    nc.vector.tensor_copy(s[:, b, :], product[:])
             return s
 
         def project_block(k, s, m, first, width):
@@ -145,7 +156,7 @@ def tile_conditionedblockattentionpairbias_b_kernel(
             rows_out = staged.tile([P, width], F32, name="rows_out")
             if m * P >= Q_ROWS + KV_ROWS:
                 nc.scalar.activation(rows_out[:], acc[:], ACT.Sigmoid)
-            elif m % 2 == 0:
+            elif m % VECTOR_COPY_EVERY == 0:
                 nc.vector.tensor_copy(rows_out[:], acc[:])
             else:
                 nc.scalar.copy(rows_out[:], acc[:])
@@ -165,7 +176,7 @@ def tile_conditionedblockattentionpairbias_b_kernel(
         for k in range(NODES // PIECE):
             last = k == NODES // PIECE - 1
             if not last:
-                x_stats = deviations_and_rstd(x_pieces[k + 1])
+                x_stats = deviations_and_rstd(x_pieces[k + 1], vector_adds_squares=True)
             project(k, s)
             if not last:
                 s = conditioned(k + 1, *x_stats)

@@ -12,19 +12,20 @@ BLOCKS = ROWS // P
 CONDS = 1024
 NODES = 2048
 PIECE = 512
+COND_WIDTHS = (PIECE // 2, PIECE // 2, PIECE)
 Q_ROWS, KV_ROWS, GATE_ROWS = 512, 1024, 512
 OUT_ROWS = Q_ROWS + KV_ROWS + GATE_ROWS
 EPS = 1e-5
 
 FLOPS = 2 * ROWS * ROWS * CONDS + 2 * ROWS * OUT_ROWS * NODES
 
-STAT_BANKS = 3
-PRODUCT_BANKS = 5
+STAT_BANKS = 2
+PRODUCT_BANKS = 6
 LAST_CUT = 4
 EARLY_PIECES = 2
+STATS_DEPTH = len(COND_WIDTHS) + 1
 WORK_DEPTH = 3
-VECTOR_COPY_EVERY = 6
-STAGED_DEPTH = PRODUCT_BANKS + 1
+STAGED_DEPTH = 2 * LAST_CUT
 
 
 def tile_conditionedblockattentionpairbias_b_kernel(
@@ -40,36 +41,41 @@ def tile_conditionedblockattentionpairbias_b_kernel(
         tc.psum_pool(name="stats", bufs=STAT_BANKS) as stats,
         tc.psum_pool(name="products", bufs=PRODUCT_BANKS) as products,
     ):
-        offsets = held.tile([P, NODES // 16], U16, name="offsets")
-        nc.sync.dma_start(offsets[:], offs)
-
         ce_rows = cond_embed.rearrange("(p a) t -> p a t", a=BLOCKS)
         ce = held.tile([P, BLOCKS, CONDS], F32, name="ce")
-        nc.sync.dma_start(ce[:, :, 0:PIECE], ce_rows[:, :, 0:PIECE])
+        cond_pieces = []
+        for width in COND_WIDTHS:
+            first = cond_pieces[-1].stop if cond_pieces else 0
+            cols = slice(first, first + width)
+            nc.sync.dma_start(ce[:, :, cols], ce_rows[:, :, cols])
+            cond_pieces.append(cols)
         ln_gain = held.tile([P, BLOCKS], F32, name="ln_gain")
         nc.scalar.dma_start(ln_gain[:], w_ln_cond.rearrange("(p a) o -> p (a o)", a=BLOCKS))
-        nc.sync.dma_start(ce[:, :, PIECE:CONDS], ce_rows[:, :, PIECE:CONDS])
-        cond_w = held.tile([P, BLOCKS, ROWS], BF16, name="cond_w")
-        nc.sync.dma_start(cond_w[:], w_cond.rearrange("(p a) c -> p a c", a=BLOCKS))
         cond_bias = held.tile([P, BLOCKS], F32, name="cond_bias")
         with nc.allow_non_contiguous_dma(reason="one bias value to a partition and block, 2 KiB in all"):
             nc.scalar.dma_start(cond_bias[:], b_cond.rearrange("(b p) o -> p (b o)", p=P))
 
         x_rows = x.rearrange("(b p) j -> p b j", p=P)
         x_pieces = []
-        proj_w = held.tile([P, BLOCKS, OUT_ROWS], BF16, name="proj_w")
-        for k in range(EARLY_PIECES):
-            x_k = nodes.tile([P, BLOCKS, PIECE], F32, name="x_k")
+
+        def load_x_piece(pool, **how):
+            k = len(x_pieces)
+            x_k = pool.tile([P, BLOCKS, PIECE], F32, name="x_k", **how)
             nc.sync.dma_start(x_k[:], x_rows[:, :, k * PIECE : (k + 1) * PIECE])
             x_pieces.append(x_k)
-            if k == 0:
-                first_row = 0
-                for w in (w_q, w_kv, w_gate):
-                    rows_of_w = w.shape[1]
-                    nc.sync.dma_start(
-                        proj_w[:, :, first_row : first_row + rows_of_w], w.rearrange("(b p) m -> p b m", p=P)
-                    )
-                    first_row += rows_of_w
+
+        load_x_piece(nodes)
+        cond_w = held.tile([P, BLOCKS, ROWS], BF16, name="cond_w")
+        nc.sync.dma_start(cond_w[:], w_cond.rearrange("(p a) c -> p a c", a=BLOCKS))
+        offsets = held.tile([P, NODES // 16], U16, name="offsets")
+        nc.sync.dma_start(offsets[:], offs)
+        load_x_piece(nodes)
+        proj_w = held.tile([P, BLOCKS, OUT_ROWS], BF16, name="proj_w")
+        first_row = 0
+        for w in (w_q, w_kv, w_gate):
+            rows_of_w = w.shape[1]
+            nc.sync.dma_start(proj_w[:, :, first_row : first_row + rows_of_w], w.rearrange("(b p) m -> p b m", p=P))
+            first_row += rows_of_w
 
         mean_w = held.tile([P, P], F32, name="mean_w")
         nc.vector.memset(mean_w[:], 1.0 / ROWS)
@@ -81,42 +87,56 @@ def tile_conditionedblockattentionpairbias_b_kernel(
         table_loaded = held.tile([P, 1], F32, name="table_loaded")
         nc.scalar.activation(table_loaded[:], eps[:], ACT.Abs_reciprocal_sqrt)
 
-        def deviations_and_rstd(rows, vector_adds_squares):
-            halves = work.tile([P, 2, PIECE], F32, name="halves")
-            nc.vector.tensor_tensor(halves[:], rows[:, 0:2, :], rows[:, 2:4, :], ALU.add)
-            total = work.tile([P, PIECE], F32, name="total")
-            nc.vector.tensor_tensor(total[:], halves[:, 0, :], halves[:, 1, :], ALU.add)
-            mean = stats.tile([P, PIECE], F32, name="stat")
-            nc.tensor.matmul(mean[:], mean_w[:], total[:], start=True, stop=True)
-            dev = work.tile([P, BLOCKS, PIECE], F32, name="dev")
-            squares = work.tile([P, BLOCKS, PIECE], BF16, name="squares")
-            var = stats.tile([P, PIECE], F32, name="stat")
+        def folded(rows, addends, name):
+            left = BLOCKS
+            while left > addends:
+                left //= 2
+                sums = work.tile([P, left, rows.shape[2]], rows.dtype, name=f"{name}{left}")
+                nc.vector.tensor_tensor(sums[:], rows[:, 0:left, :], rows[:, left : 2 * left, :], ALU.add)
+                rows = sums
+            return [rows[:, i, :] for i in range(addends)]
+
+        def column_means(weights, addends, mean):
+            for i, addend in enumerate(addends):
+                nc.tensor.matmul(mean[:], weights[:], addend, start=(i == 0), stop=(i == len(addends) - 1))
+
+        def deviations(rows, mean, addends):
+            width = rows.shape[2]
+            dev = work.tile([P, BLOCKS, width], F32, name="dev", bufs=STATS_DEPTH)
+            squares = work.tile([P, BLOCKS, width], BF16, name="squares")
+            var = stats.tile([P, width], F32, name="stat")
             for i in range(BLOCKS):
                 nc.vector.tensor_tensor(dev[:, i, :], rows[:, i, :], mean[:], ALU.subtract)
                 nc.scalar.activation(squares[:, i, :], dev[:, i, :], ACT.Square)
-                if not vector_adds_squares:
-                    nc.tensor.matmul(var[:], var_w[:], squares[:, i, :], start=(i == 0), stop=(i == BLOCKS - 1))
-            if vector_adds_squares:
-                pairs = work.tile([P, 2, PIECE], BF16, name="pairs")
-                nc.vector.tensor_tensor(pairs[:], squares[:, 0:2, :], squares[:, 2:4, :], ALU.add)
-                sum_of_squares = work.tile([P, PIECE], BF16, name="sum_of_squares")
-                nc.vector.tensor_tensor(sum_of_squares[:], pairs[:, 0, :], pairs[:, 1, :], ALU.add)
-                nc.tensor.matmul(var[:], var_w[:], sum_of_squares[:], start=True, stop=True)
-            rstd = work.tile([P, PIECE], F32, name="rstd")
-            nc.scalar.activation(rstd[:], var[:], ACT.Abs_reciprocal_sqrt, bias=eps[:])
-            return dev, rstd
+            column_means(var_w, folded(squares, addends, "squares_sum"), var)
+            return dev, var
 
-        ce_pieces = [slice(first, first + PIECE) for first in range(0, CONDS, PIECE)]
-        ce_stats = [deviations_and_rstd(ce[:, :, cols], vector_adds_squares=False) for cols in ce_pieces]
-        x_stats = deviations_and_rstd(x_pieces[0], vector_adds_squares=False)
+        def inverse_deviation(var):
+            rstd = work.tile([P, var.shape[1]], F32, name="rstd", bufs=STATS_DEPTH)
+            nc.scalar.activation(rstd[:], var[:], ACT.Abs_reciprocal_sqrt, bias=eps[:])
+            return rstd
+
+        early = [ce[:, :, cols] for cols in cond_pieces] + [x_pieces[0][:]]
+        sums = [folded(rows, 1 if i == 0 else 2, "sum") for i, rows in enumerate(early)]
+        means = [products.tile([P, rows.shape[2]], F32, name="acc") for rows in early]
+        early_stats = []
+        for i, rows in enumerate(early):
+            column_means(mean_w, sums[i], means[i])
+            early_stats.append(deviations(rows, means[i], addends=BLOCKS))
+        early_stats = [(dev, inverse_deviation(var)) for dev, var in early_stats]
+        cond_stats, x_stats = early_stats[:-1], early_stats[-1]
 
         cn = late.tile([P, BLOCKS, CONDS], BF16, tag="late", name="cn")
-        tab = [held.tile([P, CONDS], F32, name=f"tab{b}") for b in range(BLOCKS)]
-        for cols, (dev, rstd) in zip(ce_pieces, ce_stats):
+        for first in range(0, CONDS, PIECE):
             for a in range(BLOCKS):
-                nc.vector.scalar_tensor_tensor(
-                    cn[:, a, cols], dev[:, a, :], ln_gain[:, a : a + 1], rstd[:], ALU.mult, ALU.mult
-                )
+                for cols, (dev, rstd) in zip(cond_pieces, cond_stats):
+                    if first <= cols.start < first + PIECE:
+                        nc.vector.scalar_tensor_tensor(
+                            cn[:, a, cols], dev[:, a, :], ln_gain[:, a : a + 1], rstd[:], ALU.mult, ALU.mult
+                        )
+        tab = [held.tile([P, CONDS], F32, name=f"tab{b}") for b in range(BLOCKS)]
+        for first in range(0, CONDS, PIECE):
+            cols = slice(first, first + PIECE)
             for b in range(BLOCKS):
                 acc = products.tile([P, PIECE], F32, name="acc")
                 for a in range(BLOCKS):
@@ -127,9 +147,7 @@ def tile_conditionedblockattentionpairbias_b_kernel(
                 nc.scalar.activation(tab[b][:, cols], acc[:], ACT.Sigmoid, bias=cond_bias[:, b : b + 1])
 
         for k in range(EARLY_PIECES, NODES // PIECE):
-            x_k = late.tile([P, BLOCKS, PIECE], F32, tag="late", name="x_k")
-            nc.sync.dma_start(x_k[:], x_rows[:, :, k * PIECE : (k + 1) * PIECE])
-            x_pieces.append(x_k)
+            load_x_piece(late, tag="late")
 
         def conditioned(k, dev, rstd):
             piece_offsets = offsets[:, k * (PIECE // 16) : (k + 1) * (PIECE // 16)]
@@ -153,19 +171,30 @@ def tile_conditionedblockattentionpairbias_b_kernel(
                     acc[:], proj_w[:, b, m * P : (m + 1) * P], s[:, b, first : first + width],
                     start=(b == 0), stop=(b == BLOCKS - 1),
                 )
+            store_block(k, m, acc, first, width)
+
+        def store_block(k, m, acc, first, width):
             rows_out = staged.tile([P, width], F32, name="rows_out")
             if m * P >= Q_ROWS + KV_ROWS:
                 nc.scalar.activation(rows_out[:], acc[:], ACT.Sigmoid)
-            elif m % VECTOR_COPY_EVERY == 0:
-                nc.vector.tensor_copy(rows_out[:], acc[:])
             else:
                 nc.scalar.copy(rows_out[:], acc[:])
             nc.sync.dma_start(
                 out[m * P : (m + 1) * P, k * PIECE + first : k * PIECE + first + width], rows_out[:]
             )
 
-        def project(k, s):
-            for m in range(OUT_ROWS // P):
+        def project_side_by_side(k, s):
+            accs = [products.tile([P, PIECE], F32, name="acc") for m in range(PRODUCT_BANKS)]
+            for b in range(BLOCKS):
+                for m, acc in enumerate(accs):
+                    nc.tensor.matmul(
+                        acc[:], proj_w[:, b, m * P : (m + 1) * P], s[:, b, :], start=(b == 0), stop=(b == BLOCKS - 1)
+                    )
+            for m, acc in enumerate(accs):
+                store_block(k, m, acc, 0, PIECE)
+
+        def project(k, s, first_block):
+            for m in range(first_block, OUT_ROWS // P):
                 if k == NODES // PIECE - 1 and m == OUT_ROWS // P - 1:
                     for first in range(0, PIECE, PIECE // LAST_CUT):
                         project_block(k, s, m, first, PIECE // LAST_CUT)
@@ -173,10 +202,15 @@ def tile_conditionedblockattentionpairbias_b_kernel(
                     project_block(k, s, m, 0, PIECE)
 
         s = conditioned(0, *x_stats)
+        project_side_by_side(0, s)
         for k in range(NODES // PIECE):
             last = k == NODES // PIECE - 1
             if not last:
-                x_stats = deviations_and_rstd(x_pieces[k + 1], vector_adds_squares=True)
-            project(k, s)
+                sum_x = folded(x_pieces[k + 1], 1, "sum")
+                mean_x = stats.tile([P, PIECE], F32, name="stat")
+                column_means(mean_w, sum_x, mean_x)
+                dev_x, var_x = deviations(x_pieces[k + 1], mean_x, addends=2 if k == 0 else 1)
+                x_stats = dev_x, inverse_deviation(var_x)
+            project(k, s, PRODUCT_BANKS if k == 0 else 0)
             if not last:
                 s = conditioned(k + 1, *x_stats)

@@ -23,6 +23,7 @@ STAT_BANKS = 2
 PRODUCT_BANKS = 6
 LAST_CUT = 4
 EARLY_PIECES = 2
+X_AT = len(COND_WIDTHS) - 1
 STATS_DEPTH = len(COND_WIDTHS) + 1
 WORK_DEPTH = 3
 STAGED_DEPTH = 2 * LAST_CUT
@@ -36,6 +37,7 @@ def tile_conditionedblockattentionpairbias_b_kernel(
         tc.tile_pool(name="held", bufs=1) as held,
         tc.tile_pool(name="nodes", bufs=EARLY_PIECES) as nodes,
         tc.tile_pool(name="late", bufs=1) as late,
+        tc.tile_pool(name="lever", bufs=1) as lever,
         tc.tile_pool(name="work", bufs=WORK_DEPTH) as work,
         tc.tile_pool(name="staged", bufs=STAGED_DEPTH) as staged,
         tc.psum_pool(name="stats", bufs=STAT_BANKS) as stats,
@@ -44,16 +46,18 @@ def tile_conditionedblockattentionpairbias_b_kernel(
         ce_rows = cond_embed.rearrange("(p a) t -> p a t", a=BLOCKS)
         ce = held.tile([P, BLOCKS, CONDS], F32, name="ce")
         cond_pieces = []
-        for width in COND_WIDTHS:
+
+        def load_cond_piece(width):
             first = cond_pieces[-1].stop if cond_pieces else 0
             cols = slice(first, first + width)
             nc.sync.dma_start(ce[:, :, cols], ce_rows[:, :, cols])
             cond_pieces.append(cols)
+
         ln_gain = held.tile([P, BLOCKS], F32, name="ln_gain")
         nc.scalar.dma_start(ln_gain[:], w_ln_cond.rearrange("(p a) o -> p (a o)", a=BLOCKS))
-        cond_bias = held.tile([P, BLOCKS], F32, name="cond_bias")
+        bias_loaded = held.tile([P, BLOCKS], F32, name="bias_loaded")
         with nc.allow_non_contiguous_dma(reason="one bias value to a partition and block, 2 KiB in all"):
-            nc.scalar.dma_start(cond_bias[:], b_cond.rearrange("(b p) o -> p (b o)", p=P))
+            nc.scalar.dma_start(bias_loaded[:], b_cond.rearrange("(b p) o -> p (b o)", p=P))
 
         x_rows = x.rearrange("(b p) j -> p b j", p=P)
         x_pieces = []
@@ -64,7 +68,11 @@ def tile_conditionedblockattentionpairbias_b_kernel(
             nc.sync.dma_start(x_k[:], x_rows[:, :, k * PIECE : (k + 1) * PIECE])
             x_pieces.append(x_k)
 
+        for width in COND_WIDTHS[:X_AT]:
+            load_cond_piece(width)
         load_x_piece(nodes)
+        for width in COND_WIDTHS[X_AT:]:
+            load_cond_piece(width)
         cond_w = held.tile([P, BLOCKS, ROWS], BF16, name="cond_w")
         nc.sync.dma_start(cond_w[:], w_cond.rearrange("(p a) c -> p a c", a=BLOCKS))
         offsets = held.tile([P, NODES // 16], U16, name="offsets")
@@ -81,11 +89,13 @@ def tile_conditionedblockattentionpairbias_b_kernel(
         nc.vector.memset(mean_w[:], 1.0 / ROWS)
         var_w = held.tile([P, P], BF16, name="var_w")
         nc.vector.memset(var_w[:], 1.0 / ROWS)
+        eps_early = lever.tile([P, 1], F32, tag="lever", name="eps_early")
+        nc.vector.memset(eps_early[:], EPS)
         eps = held.tile([P, 1], F32, name="eps")
         nc.vector.memset(eps[:], EPS)
 
         table_loaded = held.tile([P, 1], F32, name="table_loaded")
-        nc.scalar.activation(table_loaded[:], eps[:], ACT.Abs_reciprocal_sqrt)
+        nc.scalar.activation(table_loaded[:], eps_early[:], ACT.Abs_reciprocal_sqrt)
 
         def folded(rows, addends, name):
             left = BLOCKS
@@ -95,6 +105,14 @@ def tile_conditionedblockattentionpairbias_b_kernel(
                 nc.vector.tensor_tensor(sums[:], rows[:, 0:left, :], rows[:, left : 2 * left, :], ALU.add)
                 rows = sums
             return [rows[:, i, :] for i in range(addends)]
+
+        def high_and_low(rows):
+            (total,) = folded(rows, 1, "sum")
+            high = work.tile([P, PIECE], BF16, name="high")
+            nc.vector.tensor_copy(high[:], total)
+            low = work.tile([P, PIECE], BF16, name="low")
+            nc.vector.tensor_tensor(low[:], total, high[:], ALU.subtract)
+            return [high[:], low[:]]
 
         def column_means(weights, addends, mean):
             for i, addend in enumerate(addends):
@@ -111,20 +129,23 @@ def tile_conditionedblockattentionpairbias_b_kernel(
             column_means(var_w, folded(squares, addends, "squares_sum"), var)
             return dev, var
 
-        def inverse_deviation(var):
+        def inverse_deviation(var, eps):
             rstd = work.tile([P, var.shape[1]], F32, name="rstd", bufs=STATS_DEPTH)
             nc.scalar.activation(rstd[:], var[:], ACT.Abs_reciprocal_sqrt, bias=eps[:])
             return rstd
 
-        early = [ce[:, :, cols] for cols in cond_pieces] + [x_pieces[0][:]]
-        sums = [folded(rows, 1 if i == 0 else 2, "sum") for i, rows in enumerate(early)]
+        early = [ce[:, :, cols] for cols in cond_pieces]
+        early = early[:X_AT] + [x_pieces[0]] + early[X_AT:]
+        sums = [folded(rows, 1 if rows.shape[2] < PIECE else 2, "sum") for rows in early]
         means = [products.tile([P, rows.shape[2]], F32, name="acc") for rows in early]
         early_stats = []
         for i, rows in enumerate(early):
             column_means(mean_w, sums[i], means[i])
             early_stats.append(deviations(rows, means[i], addends=BLOCKS))
-        early_stats = [(dev, inverse_deviation(var)) for dev, var in early_stats]
-        cond_stats, x_stats = early_stats[:-1], early_stats[-1]
+        early_stats = [(dev, inverse_deviation(var, eps_early)) for dev, var in early_stats]
+        cond_bias = lever.tile([P, BLOCKS], F32, tag="lever", name="cond_bias")
+        nc.scalar.copy(cond_bias[:], bias_loaded[:])
+        x_stats, cond_stats = early_stats[X_AT], early_stats[:X_AT] + early_stats[X_AT + 1 :]
 
         cn = late.tile([P, BLOCKS, CONDS], BF16, tag="late", name="cn")
         for first in range(0, CONDS, PIECE):
@@ -201,16 +222,18 @@ def tile_conditionedblockattentionpairbias_b_kernel(
                 else:
                     project_block(k, s, m, 0, PIECE)
 
+        sum_x = high_and_low(x_pieces[1])
         s = conditioned(0, *x_stats)
         project_side_by_side(0, s)
         for k in range(NODES // PIECE):
             last = k == NODES // PIECE - 1
             if not last:
-                sum_x = folded(x_pieces[k + 1], 1, "sum")
                 mean_x = stats.tile([P, PIECE], F32, name="stat")
-                column_means(mean_w, sum_x, mean_x)
-                dev_x, var_x = deviations(x_pieces[k + 1], mean_x, addends=2 if k == 0 else 1)
-                x_stats = dev_x, inverse_deviation(var_x)
+                column_means(var_w, sum_x, mean_x)
+                dev_x, var_x = deviations(x_pieces[k + 1], mean_x, addends=1)
+                x_stats = dev_x, inverse_deviation(var_x, eps)
             project(k, s, PRODUCT_BANKS if k == 0 else 0)
             if not last:
+                if k + 2 < NODES // PIECE:
+                    sum_x = high_and_low(x_pieces[k + 2])
                 s = conditioned(k + 1, *x_stats)

@@ -21,6 +21,7 @@ FLOPS = 2 * ROWS * ROWS * CONDS + 2 * ROWS * OUT_ROWS * NODES
 
 STAT_BANKS = 2
 PRODUCT_BANKS = 6
+SIDE_BY_SIDE = PRODUCT_BANKS - 1
 LAST_CUT = 4
 EARLY_PIECES = 2
 X_AT = len(COND_WIDTHS) - 1
@@ -205,7 +206,7 @@ def tile_conditionedblockattentionpairbias_b_kernel(
             )
 
         def project_side_by_side(k, s):
-            accs = [products.tile([P, PIECE], F32, name="acc") for m in range(PRODUCT_BANKS)]
+            accs = [products.tile([P, PIECE], F32, name="acc") for m in range(SIDE_BY_SIDE)]
             for b in range(BLOCKS):
                 for m, acc in enumerate(accs):
                     nc.tensor.matmul(
@@ -222,18 +223,23 @@ def tile_conditionedblockattentionpairbias_b_kernel(
                 else:
                     project_block(k, s, m, 0, PIECE)
 
-        sum_x = high_and_low(x_pieces[1])
+        def later_stats(k):
+            mean_x = stats.tile([P, PIECE], F32, name="stat")
+            if k == 1:
+                column_means(mean_w, sum_1, mean_x)
+            else:
+                column_means(var_w, high_and_low(x_pieces[k]), mean_x)
+            dev_x, var_x = deviations(x_pieces[k], mean_x, addends=1)
+            return dev_x, inverse_deviation(var_x, eps)
+
+        sum_1 = folded(x_pieces[1], 1, "sum")
         s = conditioned(0, *x_stats)
         project_side_by_side(0, s)
+        next_stats = later_stats(1)
         for k in range(NODES // PIECE):
-            last = k == NODES // PIECE - 1
-            if not last:
-                mean_x = stats.tile([P, PIECE], F32, name="stat")
-                column_means(var_w, sum_x, mean_x)
-                dev_x, var_x = deviations(x_pieces[k + 1], mean_x, addends=1)
-                x_stats = dev_x, inverse_deviation(var_x, eps)
-            project(k, s, PRODUCT_BANKS if k == 0 else 0)
-            if not last:
-                if k + 2 < NODES // PIECE:
-                    sum_x = high_and_low(x_pieces[k + 2])
+            project(k, s, SIDE_BY_SIDE if k == 0 else 0)
+            x_stats = next_stats
+            if k + 2 < NODES // PIECE:
+                next_stats = later_stats(k + 2)
+            if k + 1 < NODES // PIECE:
                 s = conditioned(k + 1, *x_stats)

@@ -22,10 +22,11 @@ FLOPS = 2 * ROWS * ROWS * CONDS + 2 * ROWS * OUT_ROWS * NODES
 STAT_BANKS = 2
 PRODUCT_BANKS = 6
 SIDE_BY_SIDE = PRODUCT_BANKS - 1
+VARIANCE_AT = 6
 LAST_CUT = 4
 EARLY_PIECES = 2
 X_AT = len(COND_WIDTHS) - 1
-STATS_DEPTH = len(COND_WIDTHS) + 1
+STATS_DEPTH = CONDS // PIECE + 1
 WORK_DEPTH = 3
 STAGED_DEPTH = 2 * LAST_CUT
 
@@ -92,8 +93,6 @@ def tile_conditionedblockattentionpairbias_b_kernel(
         nc.vector.memset(var_w[:], 1.0 / ROWS)
         eps_early = lever.tile([P, 1], F32, tag="lever", name="eps_early")
         nc.vector.memset(eps_early[:], EPS)
-        eps = held.tile([P, 1], F32, name="eps")
-        nc.vector.memset(eps[:], EPS)
 
         table_loaded = held.tile([P, 1], F32, name="table_loaded")
         nc.scalar.activation(table_loaded[:], eps_early[:], ACT.Abs_reciprocal_sqrt)
@@ -119,43 +118,46 @@ def tile_conditionedblockattentionpairbias_b_kernel(
             for i, addend in enumerate(addends):
                 nc.tensor.matmul(mean[:], weights[:], addend, start=(i == 0), stop=(i == len(addends) - 1))
 
-        def deviations(rows, mean, addends):
+        def deviations(rows, mean, addends, dev):
             width = rows.shape[2]
-            dev = work.tile([P, BLOCKS, width], F32, name="dev", bufs=STATS_DEPTH)
             squares = work.tile([P, BLOCKS, width], BF16, name="squares")
-            var = stats.tile([P, width], F32, name="stat")
             for i in range(BLOCKS):
                 nc.vector.tensor_tensor(dev[:, i, :], rows[:, i, :], mean[:], ALU.subtract)
                 nc.scalar.activation(squares[:, i, :], dev[:, i, :], ACT.Square)
-            column_means(var_w, folded(squares, addends, "squares_sum"), var)
-            return dev, var
+            return folded(squares, addends, "squares_sum")
 
-        def inverse_deviation(var, eps):
-            rstd = work.tile([P, var.shape[1]], F32, name="rstd", bufs=STATS_DEPTH)
-            nc.scalar.activation(rstd[:], var[:], ACT.Abs_reciprocal_sqrt, bias=eps[:])
-            return rstd
+        def inverse_deviation(squares, var, eps, rstd):
+            column_means(var_w, squares, var)
+            nc.scalar.activation(rstd, var[:], ACT.Abs_reciprocal_sqrt, bias=eps[:])
+
+        def stats_tiles():
+            dev = work.tile([P, BLOCKS, PIECE], F32, name="dev", bufs=STATS_DEPTH)
+            rstd = work.tile([P, PIECE], F32, name="rstd", bufs=STATS_DEPTH)
+            return dev, rstd
 
         early = [ce[:, :, cols] for cols in cond_pieces]
         early = early[:X_AT] + [x_pieces[0]] + early[X_AT:]
         sums = [folded(rows, 1 if rows.shape[2] < PIECE else 2, "sum") for rows in early]
         means = [products.tile([P, rows.shape[2]], F32, name="acc") for rows in early]
-        early_stats = []
-        for i, rows in enumerate(early):
-            column_means(mean_w, sums[i], means[i])
-            early_stats.append(deviations(rows, means[i], addends=BLOCKS))
-        early_stats = [(dev, inverse_deviation(var, eps_early)) for dev, var in early_stats]
+        halves_stats, x_stats, last_stats = stats_tiles(), stats_tiles(), stats_tiles()
+        places = [(halves_stats, cond_pieces[0]), (halves_stats, cond_pieces[1])]
+        places += [(x_stats, slice(0, PIECE)), (last_stats, slice(0, PIECE))]
+        early_squares = []
+        for rows, addends, mean, ((dev, rstd), cols) in zip(early, sums, means, places):
+            column_means(mean_w, addends, mean)
+            early_squares.append(deviations(rows, mean, BLOCKS, dev[:, :, cols]))
+        for squares, ((dev, rstd), cols) in zip(early_squares, places):
+            var = stats.tile([P, cols.stop - cols.start], F32, name="stat")
+            inverse_deviation(squares, var, eps_early, rstd[:, cols])
         cond_bias = lever.tile([P, BLOCKS], F32, tag="lever", name="cond_bias")
         nc.scalar.copy(cond_bias[:], bias_loaded[:])
-        x_stats, cond_stats = early_stats[X_AT], early_stats[:X_AT] + early_stats[X_AT + 1 :]
 
         cn = late.tile([P, BLOCKS, CONDS], BF16, tag="late", name="cn")
-        for first in range(0, CONDS, PIECE):
+        for first, (dev, rstd) in zip(range(0, CONDS, PIECE), (halves_stats, last_stats)):
             for a in range(BLOCKS):
-                for cols, (dev, rstd) in zip(cond_pieces, cond_stats):
-                    if first <= cols.start < first + PIECE:
-                        nc.vector.scalar_tensor_tensor(
-                            cn[:, a, cols], dev[:, a, :], ln_gain[:, a : a + 1], rstd[:], ALU.mult, ALU.mult
-                        )
+                nc.vector.scalar_tensor_tensor(
+                    cn[:, a, first : first + PIECE], dev[:, a, :], ln_gain[:, a : a + 1], rstd[:], ALU.mult, ALU.mult
+                )
         tab = [held.tile([P, CONDS], F32, name=f"tab{b}") for b in range(BLOCKS)]
         for first in range(0, CONDS, PIECE):
             cols = slice(first, first + PIECE)
@@ -195,10 +197,12 @@ def tile_conditionedblockattentionpairbias_b_kernel(
                 )
             store_block(k, m, acc, first, width)
 
-        def store_block(k, m, acc, first, width):
+        def store_block(k, m, acc, first, width, by_vector=False):
             rows_out = staged.tile([P, width], F32, name="rows_out")
             if m * P >= Q_ROWS + KV_ROWS:
                 nc.scalar.activation(rows_out[:], acc[:], ACT.Sigmoid)
+            elif by_vector:
+                nc.vector.tensor_copy(rows_out[:], acc[:])
             else:
                 nc.scalar.copy(rows_out[:], acc[:])
             nc.sync.dma_start(
@@ -213,33 +217,41 @@ def tile_conditionedblockattentionpairbias_b_kernel(
                         acc[:], proj_w[:, b, m * P : (m + 1) * P], s[:, b, :], start=(b == 0), stop=(b == BLOCKS - 1)
                     )
             for m, acc in enumerate(accs):
-                store_block(k, m, acc, 0, PIECE)
+                store_block(k, m, acc, 0, PIECE, by_vector=(m % 2 == 0))
 
-        def project(k, s, first_block):
-            for m in range(first_block, OUT_ROWS // P):
+        def project(k, s, blocks):
+            for m in blocks:
                 if k == NODES // PIECE - 1 and m == OUT_ROWS // P - 1:
                     for first in range(0, PIECE, PIECE // LAST_CUT):
                         project_block(k, s, m, first, PIECE // LAST_CUT)
                 else:
                     project_block(k, s, m, 0, PIECE)
 
-        def later_stats(k):
+        def later_deviations(k, sums, weights):
             mean_x = stats.tile([P, PIECE], F32, name="stat")
-            if k == 1:
-                column_means(mean_w, sum_1, mean_x)
-            else:
-                column_means(var_w, high_and_low(x_pieces[k]), mean_x)
-            dev_x, var_x = deviations(x_pieces[k], mean_x, addends=1)
-            return dev_x, inverse_deviation(var_x, eps)
+            column_means(weights, sums, mean_x)
+            dev, rstd = stats_tiles()
+            return dev, rstd, deviations(x_pieces[k], mean_x, 1, dev)
 
         sum_1 = folded(x_pieces[1], 1, "sum")
         s = conditioned(0, *x_stats)
         project_side_by_side(0, s)
-        next_stats = later_stats(1)
-        for k in range(NODES // PIECE):
-            project(k, s, SIDE_BY_SIDE if k == 0 else 0)
-            x_stats = next_stats
-            if k + 2 < NODES // PIECE:
-                next_stats = later_stats(k + 2)
-            if k + 1 < NODES // PIECE:
-                s = conditioned(k + 1, *x_stats)
+        dev, rstd, squares = later_deviations(1, sum_1, mean_w)
+        eps = lever.tile([P, 1], F32, tag="lever", name="eps")
+        nc.gpsimd.memset(eps[:], EPS)
+        table_back = held.tile([P, 1], F32, name="table_back")
+        nc.scalar.activation(table_back[:], eps[:], ACT.Abs_reciprocal_sqrt)
+        inverse_deviation(squares, stats.tile([P, PIECE], F32, name="stat"), eps, rstd[:])
+        project(0, s, range(SIDE_BY_SIDE, OUT_ROWS // P))
+        for k in range(1, NODES // PIECE):
+            last = k == NODES // PIECE - 1
+            if not last:
+                next_dev, next_rstd, squares = later_deviations(k + 1, high_and_low(x_pieces[k + 1]), var_w)
+            s = conditioned(k, dev, rstd)
+            if last:
+                project(k, s, range(OUT_ROWS // P))
+            else:
+                project(k, s, range(VARIANCE_AT))
+                dev, rstd = next_dev, next_rstd
+                inverse_deviation(squares, products.tile([P, PIECE], F32, name="acc"), eps, rstd[:])
+                project(k, s, range(VARIANCE_AT, OUT_ROWS // P))

@@ -97,12 +97,12 @@ def tile_conditionedblockattentionpairbias_b_kernel(
         table_loaded = held.tile([P, 1], F32, name="table_loaded")
         nc.scalar.activation(table_loaded[:], eps_early[:], ACT.Abs_reciprocal_sqrt)
 
-        def folded(rows, addends, name):
+        def folded(rows, addends, name, engine=nc.vector):
             left = BLOCKS
             while left > addends:
                 left //= 2
                 sums = work.tile([P, left, rows.shape[2]], rows.dtype, name=f"{name}{left}")
-                nc.vector.tensor_tensor(sums[:], rows[:, 0:left, :], rows[:, left : 2 * left, :], ALU.add)
+                engine.tensor_tensor(sums[:], rows[:, 0:left, :], rows[:, left : 2 * left, :], ALU.add)
                 rows = sums
             return [rows[:, i, :] for i in range(addends)]
 
@@ -233,7 +233,7 @@ def tile_conditionedblockattentionpairbias_b_kernel(
             dev, rstd = stats_tiles()
             return dev, rstd, deviations(x_pieces[k], mean_x, 1, dev)
 
-        sum_1 = folded(x_pieces[1], 1, "sum")
+        sum_1 = folded(x_pieces[1], 1, "sum", engine=nc.gpsimd)
         s = conditioned(0, *x_stats)
         project_side_by_side(0, s)
         dev, rstd, squares = later_deviations(1, sum_1, mean_w)

@@ -58,10 +58,9 @@ def tile_conditionedblockattentionpairbias_b_kernel(
         ln_gain = held.tile([P, BLOCKS], F32, name="ln_gain")
         nc.scalar.dma_start(ln_gain[:], w_ln_cond.rearrange("(p a) o -> p (a o)", a=BLOCKS))
         bias_loaded = held.tile([P, BLOCKS], F32, name="bias_loaded")
-        with nc.allow_non_contiguous_dma(reason="one bias value to a partition and block, 2 KiB in all"):
-            nc.scalar.dma_start(bias_loaded[:], b_cond.rearrange("(b p) o -> p (b o)", p=P))
+        nc.scalar.dma_start(bias_loaded[:], b_cond.rearrange("(p b) o -> p (b o)", b=BLOCKS))
 
-        x_rows = x.rearrange("(b p) j -> p b j", p=P)
+        x_rows = x.rearrange("(p b) j -> p b j", b=BLOCKS)
         x_pieces = []
 
         def load_x_piece(pool, **how):
@@ -84,7 +83,7 @@ def tile_conditionedblockattentionpairbias_b_kernel(
         first_row = 0
         for w in (w_q, w_kv, w_gate):
             rows_of_w = w.shape[1]
-            nc.sync.dma_start(proj_w[:, :, first_row : first_row + rows_of_w], w.rearrange("(b p) m -> p b m", p=P))
+            nc.sync.dma_start(proj_w[:, :, first_row : first_row + rows_of_w], w.rearrange("(p b) m -> p b m", b=BLOCKS))
             first_row += rows_of_w
 
         mean_w = held.tile([P, P], F32, name="mean_w")
@@ -165,7 +164,7 @@ def tile_conditionedblockattentionpairbias_b_kernel(
                 acc = products.tile([P, PIECE], F32, name="acc")
                 for a in range(BLOCKS):
                     nc.tensor.matmul(
-                        acc[:], cond_w[:, a, b * P : (b + 1) * P], cn[:, a, cols],
+                        acc[:], cond_w[:, a, b::BLOCKS], cn[:, a, cols],
                         start=(a == 0), stop=(a == BLOCKS - 1),
                     )
                 nc.scalar.activation(tab[b][:, cols], acc[:], ACT.Sigmoid, bias=cond_bias[:, b : b + 1])

@@ -16,6 +16,7 @@ COND_WIDTHS = (PIECE // 2, PIECE // 2, PIECE)
 Q_ROWS, KV_ROWS, GATE_ROWS = 512, 1024, 512
 OUT_ROWS = Q_ROWS + KV_ROWS + GATE_ROWS
 EPS = 1e-5
+VECTOR_PITCH = 8
 
 FLOPS = 2 * ROWS * ROWS * CONDS + 2 * ROWS * OUT_ROWS * NODES
 
@@ -40,6 +41,7 @@ def tile_conditionedblockattentionpairbias_b_kernel(
         tc.tile_pool(name="nodes", bufs=EARLY_PIECES) as nodes,
         tc.tile_pool(name="late", bufs=1) as late,
         tc.tile_pool(name="lever", bufs=1) as lever,
+        tc.tile_pool(name="small", bufs=1) as small,
         tc.tile_pool(name="work", bufs=WORK_DEPTH) as work,
         tc.tile_pool(name="staged", bufs=STAGED_DEPTH) as staged,
         tc.psum_pool(name="stats", bufs=STAT_BANKS) as stats,
@@ -54,11 +56,6 @@ def tile_conditionedblockattentionpairbias_b_kernel(
             cols = slice(first, first + width)
             nc.sync.dma_start(ce[:, :, cols], ce_rows[:, :, cols])
             cond_pieces.append(cols)
-
-        ln_gain = held.tile([P, BLOCKS], F32, name="ln_gain")
-        nc.scalar.dma_start(ln_gain[:], w_ln_cond.rearrange("(p a) o -> p (a o)", a=BLOCKS))
-        bias_loaded = held.tile([P, BLOCKS], F32, name="bias_loaded")
-        nc.scalar.dma_start(bias_loaded[:], b_cond.rearrange("(p b) o -> p (b o)", b=BLOCKS))
 
         x_rows = x.rearrange("(p b) j -> p b j", b=BLOCKS)
         x_pieces = []
@@ -90,11 +87,18 @@ def tile_conditionedblockattentionpairbias_b_kernel(
         nc.vector.memset(mean_w[:], 1.0 / ROWS)
         var_w = held.tile([P, P], BF16, name="var_w")
         nc.vector.memset(var_w[:], 1.0 / ROWS)
+        eps = held.tile([P, 1], F32, name="eps")
+        nc.vector.memset(eps[:], EPS)
         eps_early = lever.tile([P, 1], F32, tag="lever", name="eps_early")
         nc.vector.memset(eps_early[:], EPS)
 
-        table_loaded = held.tile([P, 1], F32, name="table_loaded")
+        table_loaded = small.tile([P, 1], F32, tag="small", name="table_loaded")
         nc.scalar.activation(table_loaded[:], eps_early[:], ACT.Abs_reciprocal_sqrt)
+
+        vectors = small.tile([P, 2, VECTOR_PITCH], F32, tag="small", name="vectors")
+        ln_gain, bias_loaded = vectors[:, 0, 0:BLOCKS], vectors[:, 1, 0:BLOCKS]
+        nc.scalar.dma_start(ln_gain, w_ln_cond.rearrange("(p a) o -> p (a o)", a=BLOCKS))
+        nc.scalar.dma_start(bias_loaded, b_cond.rearrange("(p b) o -> p (b o)", b=BLOCKS))
 
         def folded(rows, addends, name, engine=nc.vector):
             left = BLOCKS
@@ -136,7 +140,7 @@ def tile_conditionedblockattentionpairbias_b_kernel(
 
         early = [ce[:, :, cols] for cols in cond_pieces]
         early = early[:X_AT] + [x_pieces[0]] + early[X_AT:]
-        sums = [folded(rows, 1 if rows.shape[2] < PIECE else 2, "sum") for rows in early]
+        sums = [folded(rows, 1 if i <= X_AT else 2, "sum") for i, rows in enumerate(early)]
         means = [products.tile([P, rows.shape[2]], F32, name="acc") for rows in early]
         halves_stats, x_stats, last_stats = stats_tiles(), stats_tiles(), stats_tiles()
         places = [(halves_stats, cond_pieces[0]), (halves_stats, cond_pieces[1])]
@@ -149,7 +153,7 @@ def tile_conditionedblockattentionpairbias_b_kernel(
             var = stats.tile([P, cols.stop - cols.start], F32, name="stat")
             inverse_deviation(squares, var, eps_early, rstd[:, cols])
         cond_bias = lever.tile([P, BLOCKS], F32, tag="lever", name="cond_bias")
-        nc.scalar.copy(cond_bias[:], bias_loaded[:])
+        nc.scalar.copy(cond_bias[:], bias_loaded)
 
         cn = late.tile([P, BLOCKS, CONDS], BF16, tag="late", name="cn")
         for first, (dev, rstd) in zip(range(0, CONDS, PIECE), (halves_stats, last_stats)):
@@ -196,11 +200,11 @@ def tile_conditionedblockattentionpairbias_b_kernel(
                 )
             store_block(k, m, acc, first, width)
 
-        def store_block(k, m, acc, first, width, by_vector=False):
+        def store_block(k, m, acc, first, width):
             rows_out = staged.tile([P, width], F32, name="rows_out")
             if m * P >= Q_ROWS + KV_ROWS:
                 nc.scalar.activation(rows_out[:], acc[:], ACT.Sigmoid)
-            elif by_vector:
+            elif m == 0:
                 nc.vector.tensor_copy(rows_out[:], acc[:])
             else:
                 nc.scalar.copy(rows_out[:], acc[:])
@@ -216,7 +220,7 @@ def tile_conditionedblockattentionpairbias_b_kernel(
                         acc[:], proj_w[:, b, m * P : (m + 1) * P], s[:, b, :], start=(b == 0), stop=(b == BLOCKS - 1)
                     )
             for m, acc in enumerate(accs):
-                store_block(k, m, acc, 0, PIECE, by_vector=(m % 2 == 0))
+                store_block(k, m, acc, 0, PIECE)
 
         def project(k, s, blocks):
             for m in blocks:
@@ -236,10 +240,6 @@ def tile_conditionedblockattentionpairbias_b_kernel(
         s = conditioned(0, *x_stats)
         project_side_by_side(0, s)
         dev, rstd, squares = later_deviations(1, sum_1, mean_w)
-        eps = lever.tile([P, 1], F32, tag="lever", name="eps")
-        nc.gpsimd.memset(eps[:], EPS)
-        table_back = held.tile([P, 1], F32, name="table_back")
-        nc.scalar.activation(table_back[:], eps[:], ACT.Abs_reciprocal_sqrt)
         inverse_deviation(squares, stats.tile([P, PIECE], F32, name="stat"), eps, rstd[:])
         project(0, s, range(SIDE_BY_SIDE, OUT_ROWS // P))
         for k in range(1, NODES // PIECE):

@@ -140,7 +140,7 @@ def tile_conditionedblockattentionpairbias_b_kernel(
 
         early = [ce[:, :, cols] for cols in cond_pieces]
         early = early[:X_AT] + [x_pieces[0]] + early[X_AT:]
-        sums = [folded(rows, 1 if i <= X_AT else 2, "sum") for i, rows in enumerate(early)]
+        sums = [folded(rows, 1 if rows.shape[2] < PIECE else 2, "sum") for rows in early]
         means = [products.tile([P, rows.shape[2]], F32, name="acc") for rows in early]
         halves_stats, x_stats, last_stats = stats_tiles(), stats_tiles(), stats_tiles()
         places = [(halves_stats, cond_pieces[0]), (halves_stats, cond_pieces[1])]

import concourse.mybir as mybir

F32 = mybir.dt.float32
BF16 = mybir.dt.bfloat16
U16 = mybir.dt.uint16
ALU = mybir.AluOpType
ACT = mybir.ActivationFunctionType

P = 128
ROWS = 512
BLOCKS = ROWS // P
CONDS = 1024
NODES = 2048
PIECE = 512
COND_WIDTHS = (PIECE // 2, PIECE // 2, PIECE)
Q_ROWS, KV_ROWS, GATE_ROWS = 512, 1024, 512
OUT_ROWS = Q_ROWS + KV_ROWS + GATE_ROWS
EPS = 1e-5
VECTOR_PITCH = 8

FLOPS = 2 * ROWS * ROWS * CONDS + 2 * ROWS * OUT_ROWS * NODES

STAT_BANKS = 2
PRODUCT_BANKS = 6
SIDE_BY_SIDE = PRODUCT_BANKS - 1
VARIANCE_AT = 6
LAST_CUT = 4
EARLY_PIECES = 2
X_AT = len(COND_WIDTHS) - 1
STATS_DEPTH = CONDS // PIECE + 1
WORK_DEPTH = 3
STAGED_DEPTH = 2 * LAST_CUT


def tile_conditionedblockattentionpairbias_b_kernel(
    tc, x, cond_embed, w_ln_cond, w_cond, b_cond, w_q, w_kv, w_gate, offs, out
):
    nc = tc.nc
    with (
        tc.tile_pool(name="held", bufs=1) as held,
        tc.tile_pool(name="nodes", bufs=EARLY_PIECES) as nodes,
        tc.tile_pool(name="late", bufs=1) as late,
        tc.tile_pool(name="lever", bufs=1) as lever,
        tc.tile_pool(name="small", bufs=1) as small,
        tc.tile_pool(name="work", bufs=WORK_DEPTH) as work,
        tc.tile_pool(name="staged", bufs=STAGED_DEPTH) as staged,
        tc.psum_pool(name="stats", bufs=STAT_BANKS) as stats,
        tc.psum_pool(name="products", bufs=PRODUCT_BANKS) as products,
    ):
        ce_rows = cond_embed.rearrange("(p a) t -> p a t", a=BLOCKS)
        ce = held.tile([P, BLOCKS, CONDS], F32, name="ce")
        cond_pieces = []

        def load_cond_piece(width):
            first = cond_pieces[-1].stop if cond_pieces else 0
            cols = slice(first, first + width)
            nc.sync.dma_start(ce[:, :, cols], ce_rows[:, :, cols])
            cond_pieces.append(cols)

        x_rows = x.rearrange("(p b) j -> p b j", b=BLOCKS)
        x_pieces = []

        def load_x_piece(pool, **how):
            k = len(x_pieces)
            x_k = pool.tile([P, BLOCKS, PIECE], F32, name="x_k", **how)
            nc.sync.dma_start(x_k[:], x_rows[:, :, k * PIECE : (k + 1) * PIECE])
            x_pieces.append(x_k)

        for width in COND_WIDTHS[:X_AT]:
            load_cond_piece(width)
        load_x_piece(nodes)
        for width in COND_WIDTHS[X_AT:]:
            load_cond_piece(width)
        cond_w = held.tile([P, BLOCKS, ROWS], BF16, name="cond_w")
        nc.sync.dma_start(cond_w[:], w_cond.rearrange("(p a) c -> p a c", a=BLOCKS))
        offsets = held.tile([P, NODES // 16], U16, name="offsets")
        nc.sync.dma_start(offsets[:], offs)
        load_x_piece(nodes)
        proj_w = held.tile([P, BLOCKS, OUT_ROWS], BF16, name="proj_w")
        first_row = 0
        for w in (w_q, w_kv, w_gate):
            rows_of_w = w.shape[1]
            nc.sync.dma_start(proj_w[:, :, first_row : first_row + rows_of_w], w.rearrange("(p b) m -> p b m", b=BLOCKS))
            first_row += rows_of_w

        mean_w = held.tile([P, P], F32, name="mean_w")
        nc.vector.memset(mean_w[:], 1.0 / ROWS)
        var_w = held.tile([P, P], BF16, name="var_w")
        nc.vector.memset(var_w[:], 1.0 / ROWS)
        eps = held.tile([P, 1], F32, name="eps")
        nc.vector.memset(eps[:], EPS)
        eps_early = lever.tile([P, 1], F32, tag="lever", name="eps_early")
        nc.vector.memset(eps_early[:], EPS)

        table_loaded = small.tile([P, 1], F32, tag="small", name="table_loaded")
        nc.scalar.activation(table_loaded[:], eps_early[:], ACT.Abs_reciprocal_sqrt)

        vectors = small.tile([P, 2, VECTOR_PITCH], F32, tag="small", name="vectors")
        ln_gain, bias_loaded = vectors[:, 0, 0:BLOCKS], vectors[:, 1, 0:BLOCKS]
        nc.scalar.dma_start(ln_gain, w_ln_cond.rearrange("(p a) o -> p (a o)", a=BLOCKS))
        nc.scalar.dma_start(bias_loaded, b_cond.rearrange("(p b) o -> p (b o)", b=BLOCKS))

        def folded(rows, addends, name, engine=nc.vector):
            left = BLOCKS
            while left > addends:
                left //= 2
                sums = work.tile([P, left, rows.shape[2]], rows.dtype, name=f"{name}{left}")
                engine.tensor_tensor(sums[:], rows[:, 0:left, :], rows[:, left : 2 * left, :], ALU.add)
                rows = sums
            return [rows[:, i, :] for i in range(addends)]

        def high_and_low(rows):
            (total,) = folded(rows, 1, "sum")
            high = work.tile([P, PIECE], BF16, name="high")
            nc.vector.tensor_copy(high[:], total)
            low = work.tile([P, PIECE], BF16, name="low")
            nc.vector.tensor_tensor(low[:], total, high[:], ALU.subtract)
            return [high[:], low[:]]

        def column_means(weights, addends, mean):
            for i, addend in enumerate(addends):
                nc.tensor.matmul(mean[:], weights[:], addend, start=(i == 0), stop=(i == len(addends) - 1))

        def deviations(rows, mean, addends, dev):
            width = rows.shape[2]
            squares = work.tile([P, BLOCKS, width], BF16, name="squares")
            for i in range(BLOCKS):
                nc.vector.tensor_tensor(dev[:, i, :], rows[:, i, :], mean[:], ALU.subtract)
                nc.scalar.activation(squares[:, i, :], dev[:, i, :], ACT.Square)
            return folded(squares, addends, "squares_sum")

        def inverse_deviation(squares, var, eps, rstd):
            column_means(var_w, squares, var)
            nc.scalar.activation(rstd, var[:], ACT.Abs_reciprocal_sqrt, bias=eps[:])

        def stats_tiles():
            dev = work.tile([P, BLOCKS, PIECE], F32, name="dev", bufs=STATS_DEPTH)
            rstd = work.tile([P, PIECE], F32, name="rstd", bufs=STATS_DEPTH)
            return dev, rstd

        early = [ce[:, :, cols] for cols in cond_pieces]
        early = early[:X_AT] + [x_pieces[0]] + early[X_AT:]
        sums = [folded(rows, 1 if rows.shape[2] < PIECE else 2, "sum") for rows in early]
        means = [products.tile([P, rows.shape[2]], F32, name="acc") for rows in early]
        halves_stats, x_stats, last_stats = stats_tiles(), stats_tiles(), stats_tiles()
        places = [(halves_stats, cond_pieces[0]), (halves_stats, cond_pieces[1])]
        places += [(x_stats, slice(0, PIECE)), (last_stats, slice(0, PIECE))]
        early_squares = []
        for rows, addends, mean, ((dev, rstd), cols) in zip(early, sums, means, places):
            column_means(mean_w, addends, mean)
            early_squares.append(deviations(rows, mean, BLOCKS, dev[:, :, cols]))
        for squares, ((dev, rstd), cols) in zip(early_squares, places):
            var = stats.tile([P, cols.stop - cols.start], F32, name="stat")
            inverse_deviation(squares, var, eps_early, rstd[:, cols])
        cond_bias = lever.tile([P, BLOCKS], F32, tag="lever", name="cond_bias")
        nc.scalar.copy(cond_bias[:], bias_loaded)

        cn = late.tile([P, BLOCKS, CONDS], BF16, tag="late", name="cn")
        for first, (dev, rstd) in zip(range(0, CONDS, PIECE), (halves_stats, last_stats)):
            for a in range(BLOCKS):
                nc.vector.scalar_tensor_tensor(
                    cn[:, a, first : first + PIECE], dev[:, a, :], ln_gain[:, a : a + 1], rstd[:], ALU.mult, ALU.mult
                )
        tab = [held.tile([P, CONDS], F32, name=f"tab{b}") for b in range(BLOCKS)]
        for first in range(0, CONDS, PIECE):
            cols = slice(first, first + PIECE)
            for b in range(BLOCKS):
                acc = products.tile([P, PIECE], F32, name="acc")
                for a in range(BLOCKS):
                    nc.tensor.matmul(
                        acc[:], cond_w[:, a, b::BLOCKS], cn[:, a, cols],
                        start=(a == 0), stop=(a == BLOCKS - 1),
                    )
                nc.scalar.activation(tab[b][:, cols], acc[:], ACT.Sigmoid, bias=cond_bias[:, b : b + 1])

        for k in range(EARLY_PIECES, NODES // PIECE):
            load_x_piece(late, tag="late")

        def conditioned(k, dev, rstd):
            piece_offsets = offsets[:, k * (PIECE // 16) : (k + 1) * (PIECE // 16)]
            xn = work.tile([P, BLOCKS, PIECE], F32, name="xn")
            for b in range(BLOCKS):
                nc.vector.tensor_tensor(xn[:, b, :], dev[:, b, :], rstd[:], ALU.mult)
            s = work.tile([P, BLOCKS, PIECE], BF16, name="s")
            for b in range(BLOCKS):
                product = work.tile([P, PIECE], F32, name="product")
                nc.vector.tensor_tensor(product[:], tab[b][:].indirect(piece_offsets), xn[:, b, :], ALU.mult)
                if k == 0:
                    nc.scalar.copy(s[:, b, :], product[:])
                else:
                    nc.vector.tensor_copy(s[:, b, :], product[:])
            return s

        def project_block(k, s, m, first, width):
            acc = products.tile([P, width], F32, name="acc")
            for b in range(BLOCKS):
                nc.tensor.matmul(
                    acc[:], proj_w[:, b, m * P : (m + 1) * P], s[:, b, first : first + width],
                    start=(b == 0), stop=(b == BLOCKS - 1),
                )
            store_block(k, m, acc, first, width)

        def store_block(k, m, acc, first, width):
            rows_out = staged.tile([P, width], F32, name="rows_out")
            if m * P >= Q_ROWS + KV_ROWS:
                nc.scalar.activation(rows_out[:], acc[:], ACT.Sigmoid)
            elif m == 0:
                nc.vector.tensor_copy(rows_out[:], acc[:])
            else:
                nc.scalar.copy(rows_out[:], acc[:])
            nc.sync.dma_start(
                out[m * P : (m + 1) * P, k * PIECE + first : k * PIECE + first + width], rows_out[:]
            )

        def project_side_by_side(k, s):
            accs = [products.tile([P, PIECE], F32, name="acc") for m in range(SIDE_BY_SIDE)]
            for b in range(BLOCKS):
                for m, acc in enumerate(accs):
                    nc.tensor.matmul(
                        acc[:], proj_w[:, b, m * P : (m + 1) * P], s[:, b, :], start=(b == 0), stop=(b == BLOCKS - 1)
                    )
            for m, acc in enumerate(accs):
                store_block(k, m, acc, 0, PIECE)

        def project(k, s, blocks):
            for m in blocks:
                if k == NODES // PIECE - 1 and m == OUT_ROWS // P - 1:
                    for first in range(0, PIECE, PIECE // LAST_CUT):
                        project_block(k, s, m, first, PIECE // LAST_CUT)
                else:
                    project_block(k, s, m, 0, PIECE)

        def later_deviations(k, sums, weights):
            mean_x = stats.tile([P, PIECE], F32, name="stat")
            column_means(weights, sums, mean_x)
            dev, rstd = stats_tiles()
            return dev, rstd, deviations(x_pieces[k], mean_x, 1, dev)

        sum_1 = folded(x_pieces[1], 1, "sum", engine=nc.gpsimd)
        s = conditioned(0, *x_stats)
        project_side_by_side(0, s)
        dev, rstd, squares = later_deviations(1, sum_1, mean_w)
        inverse_deviation(squares, stats.tile([P, PIECE], F32, name="stat"), eps, rstd[:])
        project(0, s, range(SIDE_BY_SIDE, OUT_ROWS // P))
        for k in range(1, NODES // PIECE):
            last = k == NODES // PIECE - 1
            if not last:
                next_dev, next_rstd, squares = later_deviations(k + 1, high_and_low(x_pieces[k + 1]), var_w)
            s = conditioned(k, dev, rstd)
            if last:
                project(k, s, range(OUT_ROWS // P))
            else:
                project(k, s, range(VARIANCE_AT))
                dev, rstd = next_dev, next_rstd
                inverse_deviation(squares, products.tile([P, PIECE], F32, name="acc"), eps, rstd[:])
                project(k, s, range(VARIANCE_AT, OUT_ROWS // P))
